import numpy as np
import ml_dtypes


def mxq(x, axis, fmt="e4m3"):
    dtype, down = {"e4m3": (ml_dtypes.float8_e4m3fn, 7), "e5m2": (ml_dtypes.float8_e5m2, 14)}[fmt]
    v = np.moveaxis(np.asarray(x, np.float32).astype(ml_dtypes.bfloat16).astype(np.float64), axis, -1)
    blocks = v.reshape(v.shape[:-1] + (-1, 32))
    amax = np.abs(blocks).max(-1, keepdims=True)
    byte = np.maximum(np.where(amax > 0, np.frexp(amax)[1] - 1 + 127, 0) - down, 1)
    scale = np.exp2(byte - 127.0)
    codes = (blocks / scale).astype(np.float32).astype(dtype).astype(np.float64)
    return np.moveaxis((codes * scale).reshape(v.shape), -1, axis)


WIDE = False


def mx_kscale(k):
    if not WIDE:
        return np.ones(k)
    levels = np.array([10, -10, 5, -5, 0])
    a = np.random.permutation(np.resize(levels, k // 512 * 4)).reshape(k // 512, 4)
    idx = np.arange(k)
    return np.exp2(a[idx // 512, idx % 128 // 32])


BF16 = ml_dtypes.bfloat16


def bf(x):
    return np.asarray(x, np.float32).astype(BF16)


def f64(x):
    return np.asarray(x).astype(np.float64)


B, C, H, W, O, KH, KW = 2, 256, 31, 31, 128, 2, 2
K = C * KH * KW
STRIDE = (1, 1)
PAD = (1, 1)
DIL = (1, 1)


def _unfold(x, kh, kw, stride, padding, dilation):
    b, c, h, w = x.shape
    h_out = (h + 2 * padding[0] - dilation[0] * (kh - 1) - 1) // stride[0] + 1
    w_out = (w + 2 * padding[1] - dilation[1] * (kw - 1) - 1) // stride[1] + 1
    xp = np.pad(x, ((0, 0), (0, 0), (padding[0], padding[0]), (padding[1], padding[1])))
    rows = []
    for i in range(kh):
        for j in range(kw):
            r0 = i * dilation[0]
            c0 = j * dilation[1]
            patch = xp[:, :, r0:r0 + h_out * stride[0]:stride[0], c0:c0 + w_out * stride[1]:stride[1]]
            rows.append(patch)
    p = np.stack(rows, axis=1)
    p = p.reshape(b, kh * kw * c, h_out * w_out)
    return p, h_out, w_out


def transform_transposed_unfolded_input(inp_unf):
    return inp_unf


def setup_inputs():
    s = mx_kscale(K)[:C]
    return {"x": bf(np.random.standard_normal((B, C, H, W)) * s[None, :, None, None]),
            "weight": bf(np.random.standard_normal((O, C, KH, KW)) / np.sqrt(K) / s[None, :, None, None]),
            "bias": bf(np.random.standard_normal(O) * 0.5)}


def reference(x, weight, bias):
    x, weight, bias = f64(x), f64(weight), f64(bias)
    b = x.shape[0]
    o = weight.shape[0]
    inp_unf, h_out, w_out = _unfold(x, KH, KW, STRIDE, PAD, DIL)
    inp_t = np.ascontiguousarray(np.swapaxes(inp_unf, 1, 2))
    inp_t = transform_transposed_unfolded_input(inp_t)
    w2d = np.ascontiguousarray(weight.transpose(0, 2, 3, 1)).reshape(o, -1)
    out_lo = mxq(inp_t, 2, "e4m3") @ mxq(w2d, 1, "e4m3").T
    out_unf = np.swapaxes(out_lo, 1, 2)
    out = out_unf.reshape(b, o, h_out, w_out)
    out = out + bias.reshape(1, o, 1, 1)
    return out

@@ -1,0 +1,123 @@
+import concourse.mybir as mybir
+from concourse.masks import make_identity
+
+BF16 = mybir.dt.bfloat16
+F32 = mybir.dt.float32
+I32 = mybir.dt.int32
+U32 = mybir.dt.uint32
+U8 = mybir.dt.uint8
+FP8X4 = mybir.dt.float8_e4m3fn_x4
+
+P = 128
+B, C, H, W = 2, 256, 31, 31
+O, KH, KW = 128, 2, 2
+HO, WO = 32, 32
+E = C // P
+PACK = KW * E
+ROW = B * WO
+CHUNK = 8
+N_CHUNKS = HO // CHUNK
+N_TILE = CHUNK * ROW
+
+FLOPS = 2 * B * HO * WO * C * KH * KW * O
+
+
+def tile_customconvmodule_s_kernel(tc, x, weight, bias, out):
+    nc = tc.nc
+    with tc.tile_pool(name="keep", bufs=1) as keep, tc.tile_pool(
+        name="results", bufs=N_CHUNKS
+    ) as results, tc.psum_pool(name="turned", bufs=1) as turned, tc.psum_pool(
+        name="sums", bufs=N_CHUNKS
+    ) as sums:
+        w_rows = keep.tile([O, C * KH * KW], BF16)
+        nc.sync.dma_start(out=w_rows[:], in_=weight.rearrange("o c i j -> o (c i j)"))
+        raw = []
+        for v in range(N_CHUNKS):
+            h0 = v * CHUNK
+            rows = min(CHUNK, H - h0)
+            raw_v = keep.tile([P, B, E, CHUNK * W], BF16, name="raw%d" % v)
+            for b in range(B):
+                nc.sync.dma_start(
+                    out=raw_v[:, b, :, 0 : rows * W],
+                    in_=x[b].rearrange("(p e) h w -> p e (h w)", e=E)[:, :, h0 * W : (h0 + rows) * W],
+                )
+            raw.append(raw_v)
+        bias_rows = keep.tile([P, P], BF16)
+        nc.vector.memset(bias_rows[:], 0.0)
+        nc.scalar.dma_start(out=bias_rows[0:1, :], in_=bias.rearrange("(u o) -> u o", u=1))
+
+        ident = keep.tile([P, P], BF16)
+        make_identity(nc, ident[:])
+
+        grouped = keep.tile([P, HO, B, WO * PACK], BF16, align_bytes=64)
+        edge = 16
+        nc.vector.memset(grouped[:, :, :, 0:edge], 0.0)
+        nc.vector.memset(grouped[:, :, :, WO * PACK - edge : WO * PACK], 0.0)
+        nc.vector.memset(grouped[:, H, :, :], 0.0)
+        x_codes = keep.tile([P, (HO + 1) * ROW], U32, align_bytes=64)
+        x_scales = keep.tile([P, (HO + 1) * ROW], U8, align_bytes=64)
+        nc.vector.memset(x_codes[:, 0:ROW].bitcast(I32), 0)
+        nc.vector.memset(x_scales[:, 0:ROW].bitcast(I32), 0)
+
+        w_by_tap = w_rows[:].rearrange("o (p e i j) -> o e i j p", e=E, i=KH, j=KW)
+        w_grouped = keep.tile([P, KH, O, KW, E], BF16, align_bytes=64)
+        for i in range(KH):
+            w_turned = turned.tile([P, KW, E, O], BF16, name="w_turned%d" % i)
+            for j in range(KW):
+                for e in range(E):
+                    nc.tensor.transpose(w_turned[:, j, e, :], w_by_tap[:, e, i, j, :], ident[:])
+            copy = nc.vector.tensor_copy if i == 0 else nc.scalar.copy
+            copy(out=w_grouped[:, i], in_=w_turned[:].rearrange("p j e o -> p o j e"))
+        bias_turned = turned.tile([P, P], BF16)
+        nc.tensor.transpose(bias_turned[:], bias_rows[:], ident[:])
+        bias_col = keep.tile([P, 1], F32)
+        nc.vector.tensor_copy(out=bias_col[:], in_=bias_turned[:, 0:1])
+        w_codes = keep.tile([P, KH * O], U32, align_bytes=64)
+        w_scales = keep.tile([P, KH * O], U8, align_bytes=64)
+        nc.vector.quantize_mx(
+            out=w_codes[:].bitcast(FP8X4),
+            scales=w_scales[:],
+            in_=w_grouped[:].rearrange("p i o j e -> p (i o j e)"),
+        )
+
+        for v in range(N_CHUNKS):
+            h0 = v * CHUNK
+            rows = min(CHUNK, H - h0)
+            for b in range(B):
+                source = raw[v][:, b, :, 0 : rows * W].rearrange("p e (h w) -> p h w e", w=W)
+                copy = nc.vector.tensor_copy if b == 0 else nc.scalar.copy
+                copy(
+                    out=grouped[:, h0 : h0 + rows, b, E : E + W * PACK].rearrange(
+                        "p h (w d e) -> p h w d e", d=KW, e=E
+                    ),
+                    in_=source.unsqueeze(3).to_broadcast([P, rows, W, KW, E]),
+                )
+            first = (h0 + 1) * ROW
+            nc.vector.quantize_mx(
+                out=x_codes[:, first : first + N_TILE].bitcast(FP8X4),
+                scales=x_scales[:, first : first + N_TILE],
+                in_=grouped[:, h0 : h0 + CHUNK].rearrange("p h b f -> p (h b f)"),
+            )
+            acc = sums.tile([O, N_TILE], F32)
+            for i in range(KH):
+                window = slice((h0 + i) * ROW, (h0 + i) * ROW + N_TILE)
+                nc.tensor.matmul_mx(
+                    out=acc[:],
+                    lhsT=w_codes[:, i * O : (i + 1) * O].bitcast(FP8X4),
+                    lhsT_scale=w_scales[:, i * O : (i + 1) * O],
+                    rhs=x_codes[:, window].bitcast(FP8X4),
+                    rhs_scale=x_scales[:, window],
+                    start=(i == 0),
+                    stop=(i == KH - 1),
+                )
+            result = results.tile([O, B, CHUNK, WO], F32)
+            nc.scalar.activation(
+                out=result[:],
+                in_=acc[:].rearrange("o (y b z) -> o b y z", b=B, z=WO),
+                func=mybir.ActivationFunctionType.Identity,
+                bias=bias_col[:, 0:1],
+            )
+            nc.sync.dma_start(
+                out=out.rearrange("b o y z -> o b (y z)")[:, :, h0 * WO : (h0 + CHUNK) * WO],
+                in_=result[:].rearrange("o b y z -> o b (y z)"),
+            )

@@ -18,6 +18,7 @@ ROW = B * WO
 CHUNK = 8
 N_CHUNKS = HO // CHUNK
 N_TILE = CHUNK * ROW
+EDGE = 16
 
 FLOPS = 2 * B * HO * WO * C * KH * KW * O
 
@@ -28,77 +29,57 @@ def tile_customconvmodule_s_kernel(tc, x, weight, bias, out):
         name="results", bufs=N_CHUNKS
     ) as results, tc.psum_pool(name="turned", bufs=1) as turned, tc.psum_pool(
         name="sums", bufs=N_CHUNKS
-    ) as sums:
+    ) as sums, tc.manual_schedule():
+        raw = [keep.tile([P, B, E, CHUNK * W], BF16, name="raw%d" % v) for v in range(N_CHUNKS)]
         w_rows = keep.tile([O, C * KH * KW], BF16)
-        nc.sync.dma_start(out=w_rows[:], in_=weight.rearrange("o c i j -> o (c i j)"))
-        raw = []
-        for v in range(N_CHUNKS):
-            h0 = v * CHUNK
-            rows = min(CHUNK, H - h0)
-            raw_v = keep.tile([P, B, E, CHUNK * W], BF16, name="raw%d" % v)
-            for b in range(B):
-                nc.sync.dma_start(
-                    out=raw_v[:, b, :, 0 : rows * W],
-                    in_=x[b].rearrange("(p e) h w -> p e (h w)", e=E)[:, :, h0 * W : (h0 + rows) * W],
-                )
-            raw.append(raw_v)
         bias_rows = keep.tile([P, P], BF16)
-        nc.vector.memset(bias_rows[:], 0.0)
-        nc.scalar.dma_start(out=bias_rows[0:1, :], in_=bias.rearrange("(u o) -> u o", u=1))
-
         ident = keep.tile([P, P], BF16)
-        make_identity(nc, ident[:])
-
+        warm = keep.tile([P, 1], F32)
         grouped = keep.tile([P, HO, B, WO * PACK], BF16, align_bytes=64)
-        edge = 16
-        nc.vector.memset(grouped[:, :, :, 0:edge], 0.0)
-        nc.vector.memset(grouped[:, :, :, WO * PACK - edge : WO * PACK], 0.0)
-        nc.vector.memset(grouped[:, H, :, :], 0.0)
         x_codes = keep.tile([P, (HO + 1) * ROW], U32, align_bytes=64)
         x_scales = keep.tile([P, (HO + 1) * ROW], U8, align_bytes=64)
-        nc.vector.memset(x_codes[:, 0:ROW].bitcast(I32), 0)
-        nc.vector.memset(x_scales[:, 0:ROW].bitcast(I32), 0)
-
-        w_by_tap = w_rows[:].rearrange("o (p e i j) -> o e i j p", e=E, i=KH, j=KW)
         w_grouped = keep.tile([P, KH, O, KW, E], BF16, align_bytes=64)
-        for i in range(KH):
-            w_turned = turned.tile([P, KW, E, O], BF16, name="w_turned%d" % i)
-            for j in range(KW):
-                for e in range(E):
-                    nc.tensor.transpose(w_turned[:, j, e, :], w_by_tap[:, e, i, j, :], ident[:])
-            copy = nc.vector.tensor_copy if i == 0 else nc.scalar.copy
-            copy(out=w_grouped[:, i], in_=w_turned[:].rearrange("p j e o -> p o j e"))
-        bias_turned = turned.tile([P, P], BF16)
-        nc.tensor.transpose(bias_turned[:], bias_rows[:], ident[:])
-        bias_col = keep.tile([P, 1], F32)
-        nc.vector.tensor_copy(out=bias_col[:], in_=bias_turned[:, 0:1])
         w_codes = keep.tile([P, KH * O], U32, align_bytes=64)
         w_scales = keep.tile([P, KH * O], U8, align_bytes=64)
-        nc.vector.quantize_mx(
-            out=w_codes[:].bitcast(FP8X4),
-            scales=w_scales[:],
-            in_=w_grouped[:].rearrange("p i o j e -> p (i o j e)"),
-        )
+        bias_col = keep.tile([P, 1], F32)
 
-        for v in range(N_CHUNKS):
-            h0 = v * CHUNK
-            rows = min(CHUNK, H - h0)
+        def rows_of(v):
+            return min(CHUNK, H - v * CHUNK)
+
+        def load(v):
+            first = v * CHUNK * W
             for b in range(B):
+                nc.sync.dma_start(
+                    out=raw[v][:, b, :, 0 : rows_of(v) * W],
+                    in_=x[b].rearrange("(p e) h w -> p e (h w)", e=E)[:, :, first : first + rows_of(v) * W],
+                )
+
+        def regroup(v):
+            h0 = v * CHUNK
+            rows = rows_of(v)
+            for b in range(B):
+                scalar_helps = b == 1 and 0 < v < N_CHUNKS - 1
+                copy = nc.scalar.copy if scalar_helps else nc.vector.tensor_copy
                 source = raw[v][:, b, :, 0 : rows * W].rearrange("p e (h w) -> p h w e", w=W)
-                copy = nc.vector.tensor_copy if b == 0 else nc.scalar.copy
                 copy(
                     out=grouped[:, h0 : h0 + rows, b, E : E + W * PACK].rearrange(
                         "p h (w d e) -> p h w d e", d=KW, e=E
                     ),
                     in_=source.unsqueeze(3).to_broadcast([P, rows, W, KW, E]),
                 )
+
+        def quantise(v):
+            h0 = v * CHUNK
             first = (h0 + 1) * ROW
             nc.vector.quantize_mx(
                 out=x_codes[:, first : first + N_TILE].bitcast(FP8X4),
                 scales=x_scales[:, first : first + N_TILE],
                 in_=grouped[:, h0 : h0 + CHUNK].rearrange("p h b f -> p (h b f)"),
             )
-            acc = sums.tile([O, N_TILE], F32)
+
+        def multiply_and_store(v):
+            h0 = v * CHUNK
+            acc = sums.tile([O, N_TILE], F32, name="acc")
             for i in range(KH):
                 window = slice((h0 + i) * ROW, (h0 + i) * ROW + N_TILE)
                 nc.tensor.matmul_mx(
@@ -110,7 +91,7 @@ def tile_customconvmodule_s_kernel(tc, x, weight, bias, out):
                     start=(i == 0),
                     stop=(i == KH - 1),
                 )
-            result = results.tile([O, B, CHUNK, WO], F32)
+            result = results.tile([O, B, CHUNK, WO], F32, name="result")
             nc.scalar.activation(
                 out=result[:],
                 in_=acc[:].rearrange("o (y b z) -> o b y z", b=B, z=WO),
@@ -121,3 +102,49 @@ def tile_customconvmodule_s_kernel(tc, x, weight, bias, out):
                 out=out.rearrange("b o y z -> o b (y z)")[:, :, h0 * WO : (h0 + CHUNK) * WO],
                 in_=result[:].rearrange("o b y z -> o b (y z)"),
             )
+
+        load(0)
+        nc.sync.dma_start(out=w_rows[:], in_=weight.rearrange("o c i j -> o (c i j)"))
+        for v in range(1, N_CHUNKS):
+            load(v)
+        nc.vector.memset(bias_rows[:], 0.0)
+        nc.scalar.dma_start(out=bias_rows[0:1, :], in_=bias.rearrange("(u o) -> u o", u=1))
+
+        nc.vector.memset(warm[:], 0.0)
+        nc.scalar.activation(out=warm[:], in_=warm[:], func=mybir.ActivationFunctionType.Identity)
+        make_identity(nc, ident[:])
+        nc.vector.memset(grouped[:, :, :, 0:EDGE], 0.0)
+        nc.vector.memset(grouped[:, :, :, WO * PACK - EDGE : WO * PACK], 0.0)
+        nc.vector.memset(grouped[:, H, :, :], 0.0)
+        nc.vector.memset(x_codes[:, 0:ROW].bitcast(I32), 0)
+        nc.vector.memset(x_scales[:, 0:ROW].bitcast(I32), 0)
+
+        w_by_tap = w_rows[:].rearrange("o (p e i j) -> o e i j p", e=E, i=KH, j=KW)
+        w_turned = [turned.tile([P, KW, E, O], BF16, name="w_turned%d" % i) for i in range(KH)]
+        for i in range(KH):
+            for j in range(KW):
+                for e in range(E):
+                    nc.tensor.transpose(w_turned[i][:, j, e, :], w_by_tap[:, e, i, j, :], ident[:])
+        bias_turned = turned.tile([P, P], BF16)
+        nc.tensor.transpose(bias_turned[:], bias_rows[:], ident[:])
+
+        regroup(0)
+        regroup(1)
+        quantise(0)
+        regroup(2)
+        quantise(1)
+        for i in range(KH):
+            nc.scalar.copy(out=w_grouped[:, i], in_=w_turned[i][:].rearrange("p j e o -> p o j e"))
+        nc.scalar.copy(out=bias_col[:], in_=bias_turned[:, 0:1])
+        regroup(3)
+        nc.vector.quantize_mx(
+            out=w_codes[:].bitcast(FP8X4),
+            scales=w_scales[:],
+            in_=w_grouped[:].rearrange("p i o j e -> p (i o j e)"),
+        )
+        multiply_and_store(0)
+        multiply_and_store(1)
+        quantise(2)
+        multiply_and_store(2)
+        quantise(3)
+        multiply_and_store(3)

@@ -21,14 +21,16 @@ N_TILE = CHUNK * ROW
 EDGE = 16
 
 FLOPS = 2 * B * HO * WO * C * KH * KW * O
+SCALAR_CHUNKS = 2
+STEPS = [(0, 8), (8, 8), (16, 8), (24, 4), (28, 4)]
 
 
 def tile_customconvmodule_s_kernel(tc, x, weight, bias, out):
     nc = tc.nc
     with tc.tile_pool(name="keep", bufs=1) as keep, tc.tile_pool(
-        name="results", bufs=N_CHUNKS
+        name="results", bufs=len(STEPS)
     ) as results, tc.psum_pool(name="turned", bufs=1) as turned, tc.psum_pool(
-        name="sums", bufs=N_CHUNKS
+        name="sums", bufs=4
     ) as sums, tc.manual_schedule():
         raw = [keep.tile([P, B, E, CHUNK * W], BF16, name="raw%d" % v) for v in range(N_CHUNKS)]
         w_rows = keep.tile([O, C * KH * KW], BF16)
@@ -51,15 +53,14 @@ def tile_customconvmodule_s_kernel(tc, x, weight, bias, out):
             for b in range(B):
                 nc.sync.dma_start(
                     out=raw[v][:, b, :, 0 : rows_of(v) * W],
-                    in_=x[b].rearrange("(p e) h w -> p e (h w)", e=E)[:, :, first : first + rows_of(v) * W],
+                    in_=x[b].rearrange("(e p) h w -> p e (h w)", e=E)[:, :, first : first + rows_of(v) * W],
                 )
 
         def regroup(v):
             h0 = v * CHUNK
             rows = rows_of(v)
             for b in range(B):
-                scalar_helps = b == 1 and 0 < v < N_CHUNKS - 1
-                copy = nc.scalar.copy if scalar_helps else nc.vector.tensor_copy
+                copy = nc.scalar.copy if b == 1 and v < SCALAR_CHUNKS else nc.vector.tensor_copy
                 source = raw[v][:, b, :, 0 : rows * W].rearrange("p e (h w) -> p h w e", w=W)
                 copy(
                     out=grouped[:, h0 : h0 + rows, b, E : E + W * PACK].rearrange(
@@ -68,20 +69,18 @@ def tile_customconvmodule_s_kernel(tc, x, weight, bias, out):
                     in_=source.unsqueeze(3).to_broadcast([P, rows, W, KW, E]),
                 )
 
-        def quantise(v):
-            h0 = v * CHUNK
+        def quantise(h0, rows):
             first = (h0 + 1) * ROW
             nc.vector.quantize_mx(
-                out=x_codes[:, first : first + N_TILE].bitcast(FP8X4),
-                scales=x_scales[:, first : first + N_TILE],
-                in_=grouped[:, h0 : h0 + CHUNK].rearrange("p h b f -> p (h b f)"),
+                out=x_codes[:, first : first + rows * ROW].bitcast(FP8X4),
+                scales=x_scales[:, first : first + rows * ROW],
+                in_=grouped[:, h0 : h0 + rows].rearrange("p h b f -> p (h b f)"),
             )
 
-        def multiply_and_store(v):
-            h0 = v * CHUNK
-            acc = sums.tile([O, N_TILE], F32, name="acc")
+        def multiply_and_store(h0, rows):
+            acc = sums.tile([O, rows * ROW], F32, name="acc")
             for i in range(KH):
-                window = slice((h0 + i) * ROW, (h0 + i) * ROW + N_TILE)
+                window = slice((h0 + i) * ROW, (h0 + i + rows) * ROW)
                 nc.tensor.matmul_mx(
                     out=acc[:],
                     lhsT=w_codes[:, i * O : (i + 1) * O].bitcast(FP8X4),
@@ -91,7 +90,7 @@ def tile_customconvmodule_s_kernel(tc, x, weight, bias, out):
                     start=(i == 0),
                     stop=(i == KH - 1),
                 )
-            result = results.tile([O, B, CHUNK, WO], F32, name="result")
+            result = results.tile([O, B, rows, WO], F32, name="result")
             nc.scalar.activation(
                 out=result[:],
                 in_=acc[:].rearrange("o (y b z) -> o b y z", b=B, z=WO),
@@ -99,13 +98,12 @@ def tile_customconvmodule_s_kernel(tc, x, weight, bias, out):
                 bias=bias_col[:, 0:1],
             )
             nc.sync.dma_start(
-                out=out.rearrange("b o y z -> o b (y z)")[:, :, h0 * WO : (h0 + CHUNK) * WO],
+                out=out.rearrange("b o y z -> o b (y z)")[:, :, h0 * WO : (h0 + rows) * WO],
                 in_=result[:].rearrange("o b y z -> o b (y z)"),
             )
 
-        load(0)
         nc.sync.dma_start(out=w_rows[:], in_=weight.rearrange("o c i j -> o (c i j)"))
-        for v in range(1, N_CHUNKS):
+        for v in range(N_CHUNKS):
             load(v)
         nc.vector.memset(bias_rows[:], 0.0)
         nc.scalar.dma_start(out=bias_rows[0:1, :], in_=bias.rearrange("(u o) -> u o", u=1))
@@ -119,7 +117,7 @@ def tile_customconvmodule_s_kernel(tc, x, weight, bias, out):
         nc.vector.memset(x_codes[:, 0:ROW].bitcast(I32), 0)
         nc.vector.memset(x_scales[:, 0:ROW].bitcast(I32), 0)
 
-        w_by_tap = w_rows[:].rearrange("o (p e i j) -> o e i j p", e=E, i=KH, j=KW)
+        w_by_tap = w_rows[:].rearrange("o (e p i j) -> o e i j p", e=E, i=KH, j=KW)
         w_turned = [turned.tile([P, KW, E, O], BF16, name="w_turned%d" % i) for i in range(KH)]
         for i in range(KH):
             for j in range(KW):
@@ -128,23 +126,30 @@ def tile_customconvmodule_s_kernel(tc, x, weight, bias, out):
         bias_turned = turned.tile([P, P], BF16)
         nc.tensor.transpose(bias_turned[:], bias_rows[:], ident[:])
 
+        def copy_weight_out():
+            for i in range(KH):
+                nc.scalar.copy(out=w_grouped[:, i], in_=w_turned[i][:].rearrange("p j e o -> p o j e"))
+            nc.scalar.copy(out=bias_col[:], in_=bias_turned[:, 0:1])
+
+        def quantise_weight():
+            nc.vector.quantize_mx(
+                out=w_codes[:].bitcast(FP8X4),
+                scales=w_scales[:],
+                in_=w_grouped[:].rearrange("p i o j e -> p (i o j e)"),
+            )
+
         regroup(0)
+        copy_weight_out()
         regroup(1)
-        quantise(0)
+        quantise(*STEPS[0])
         regroup(2)
-        quantise(1)
-        for i in range(KH):
-            nc.scalar.copy(out=w_grouped[:, i], in_=w_turned[i][:].rearrange("p j e o -> p o j e"))
-        nc.scalar.copy(out=bias_col[:], in_=bias_turned[:, 0:1])
+        quantise_weight()
+        multiply_and_store(*STEPS[0])
+        quantise(*STEPS[1])
+        multiply_and_store(*STEPS[1])
+        quantise(*STEPS[2])
+        multiply_and_store(*STEPS[2])
         regroup(3)
-        nc.vector.quantize_mx(
-            out=w_codes[:].bitcast(FP8X4),
-            scales=w_scales[:],
-            in_=w_grouped[:].rearrange("p i o j e -> p (i o j e)"),
-        )
-        multiply_and_store(0)
-        multiply_and_store(1)
-        quantise(2)
-        multiply_and_store(2)
-        quantise(3)
-        multiply_and_store(3)
+        for step in STEPS[3:]:
+            quantise(*step)
+            multiply_and_store(*step)

@@ -21,7 +21,6 @@ N_TILE = CHUNK * ROW
 EDGE = 16
 
 FLOPS = 2 * B * HO * WO * C * KH * KW * O
-SCALAR_CHUNKS = 2
 STEPS = [(0, 8), (8, 8), (16, 8), (24, 4), (28, 4)]
 
 
@@ -56,18 +55,17 @@ def tile_customconvmodule_s_kernel(tc, x, weight, bias, out):
                     in_=x[b].rearrange("(e p) h w -> p e (h w)", e=E)[:, :, first : first + rows_of(v) * W],
                 )
 
-        def regroup(v):
+        def regroup(v, b):
             h0 = v * CHUNK
             rows = rows_of(v)
-            for b in range(B):
-                copy = nc.scalar.copy if b == 1 and v < SCALAR_CHUNKS else nc.vector.tensor_copy
-                source = raw[v][:, b, :, 0 : rows * W].rearrange("p e (h w) -> p h w e", w=W)
-                copy(
-                    out=grouped[:, h0 : h0 + rows, b, E : E + W * PACK].rearrange(
-                        "p h (w d e) -> p h w d e", d=KW, e=E
-                    ),
-                    in_=source.unsqueeze(3).to_broadcast([P, rows, W, KW, E]),
-                )
+            copy = nc.scalar.copy if b == 1 and 0 < v < N_CHUNKS - 1 else nc.vector.tensor_copy
+            source = raw[v][:, b, :, 0 : rows * W].rearrange("p e (h w) -> p h w e", w=W)
+            copy(
+                out=grouped[:, h0 : h0 + rows, b, E : E + W * PACK].rearrange(
+                    "p h (w d e) -> p h w d e", d=KW, e=E
+                ),
+                in_=source.unsqueeze(3).to_broadcast([P, rows, W, KW, E]),
+            )
 
         def quantise(h0, rows):
             first = (h0 + 1) * ROW
@@ -138,18 +136,17 @@ def tile_customconvmodule_s_kernel(tc, x, weight, bias, out):
                 in_=w_grouped[:].rearrange("p i o j e -> p (i o j e)"),
             )
 
-        regroup(0)
-        copy_weight_out()
-        regroup(1)
-        quantise(*STEPS[0])
-        regroup(2)
-        quantise_weight()
-        multiply_and_store(*STEPS[0])
-        quantise(*STEPS[1])
-        multiply_and_store(*STEPS[1])
-        quantise(*STEPS[2])
-        multiply_and_store(*STEPS[2])
-        regroup(3)
-        for step in STEPS[3:]:
-            quantise(*step)
-            multiply_and_store(*step)
+        for v in range(N_CHUNKS + 1):
+            if v < N_CHUNKS:
+                regroup(v, 0)
+            for h0, rows in STEPS:
+                if h0 // CHUNK == v - 1:
+                    quantise(h0, rows)
+            if v == 0:
+                copy_weight_out()
+            if v == 1:
+                quantise_weight()
+            if v < N_CHUNKS:
+                regroup(v, 1)
+        for h0, rows in STEPS:
+            multiply_and_store(h0, rows)

@@ -33,8 +33,9 @@ def tile_customconvmodule_s_kernel(tc, x, weight, bias, out):
     ) as sums, tc.manual_schedule():
         raw = [keep.tile([P, B, E, CHUNK * W], BF16, name="raw%d" % v) for v in range(N_CHUNKS)]
         w_rows = keep.tile([O, C * KH * KW], BF16)
-        bias_rows = keep.tile([P, P], BF16)
-        ident = keep.tile([P, P], BF16)
+        bias_row = keep.tile([1, O], BF16)
+        bias_rows = keep.tile([P, P], F32)
+        ident = keep.tile([P, P], F32)
         warm = keep.tile([P, 1], F32)
         grouped = keep.tile([P, HO, B, WO * PACK], BF16, align_bytes=64)
         x_codes = keep.tile([P, (HO + 1) * ROW], U32, align_bytes=64)
@@ -104,29 +105,29 @@ def tile_customconvmodule_s_kernel(tc, x, weight, bias, out):
         for v in range(N_CHUNKS):
             load(v)
         nc.vector.memset(bias_rows[:], 0.0)
-        nc.scalar.dma_start(out=bias_rows[0:1, :], in_=bias.rearrange("(u o) -> u o", u=1))
+        nc.scalar.dma_start(out=bias_row[:], in_=bias.rearrange("(u o) -> u o", u=1))
 
         nc.vector.memset(warm[:], 0.0)
         nc.scalar.activation(out=warm[:], in_=warm[:], func=mybir.ActivationFunctionType.Identity)
         make_identity(nc, ident[:])
+        nc.gpsimd.tensor_copy(out=bias_rows[0:1, :], in_=bias_row[:])
         nc.vector.memset(grouped[:, :, :, 0:EDGE], 0.0)
         nc.vector.memset(grouped[:, :, :, WO * PACK - EDGE : WO * PACK], 0.0)
         nc.vector.memset(grouped[:, H, :, :], 0.0)
         nc.vector.memset(x_codes[:, 0:ROW].bitcast(I32), 0)
         nc.vector.memset(x_scales[:, 0:ROW].bitcast(I32), 0)
 
-        w_by_tap = w_rows[:].rearrange("o (e p i j) -> o e i j p", e=E, i=KH, j=KW)
-        w_turned = [turned.tile([P, KW, E, O], BF16, name="w_turned%d" % i) for i in range(KH)]
+        w_pairs = w_rows[:].bitcast(F32).rearrange("o (e p i) -> o e i p", e=E, i=KH)
+        w_turned = [turned.tile([P, E, O], F32, name="w_turned%d" % i) for i in range(KH)]
         for i in range(KH):
-            for j in range(KW):
-                for e in range(E):
-                    nc.tensor.transpose(w_turned[i][:, j, e, :], w_by_tap[:, e, i, j, :], ident[:])
-        bias_turned = turned.tile([P, P], BF16)
+            for e in range(E):
+                nc.tensor.transpose(w_turned[i][:, e, :], w_pairs[:, e, i, :], ident[:])
+        bias_turned = turned.tile([P, P], F32)
         nc.tensor.transpose(bias_turned[:], bias_rows[:], ident[:])
 
         def copy_weight_out():
             for i in range(KH):
-                nc.scalar.copy(out=w_grouped[:, i], in_=w_turned[i][:].rearrange("p j e o -> p o j e"))
+                nc.scalar.copy(out=w_grouped[:, i], in_=w_turned[i][:].bitcast(BF16).rearrange("p e (o j) -> p o j e", j=KW))
             nc.scalar.copy(out=bias_col[:], in_=bias_turned[:, 0:1])
 
         def quantise_weight():

@@ -18,7 +18,7 @@ ROW = B * WO
 CHUNK = 8
 N_CHUNKS = HO // CHUNK
 N_TILE = CHUNK * ROW
-EDGE = 16
+HALF = WO // 2
 
 FLOPS = 2 * B * HO * WO * C * KH * KW * O
 STEPS = [(0, 8), (8, 8), (16, 8), (24, 4), (28, 4)]
@@ -37,10 +37,10 @@ def tile_customconvmodule_s_kernel(tc, x, weight, bias, out):
         bias_rows = keep.tile([P, P], F32)
         ident = keep.tile([P, P], F32)
         warm = keep.tile([P, 1], F32)
-        grouped = keep.tile([P, HO, B, WO * PACK], BF16, align_bytes=64)
+        grouped = keep.tile([P, HO, B, KW, HALF, E, KW], BF16, align_bytes=64)
         x_codes = keep.tile([P, (HO + 1) * ROW], U32, align_bytes=64)
         x_scales = keep.tile([P, (HO + 1) * ROW], U8, align_bytes=64)
-        w_grouped = keep.tile([P, KH, O, KW, E], BF16, align_bytes=64)
+        w_grouped = keep.tile([P, KH, O, E, KW], BF16, align_bytes=64)
         w_codes = keep.tile([P, KH * O], U32, align_bytes=64)
         w_scales = keep.tile([P, KH * O], U8, align_bytes=64)
         bias_col = keep.tile([P, 1], F32)
@@ -59,21 +59,24 @@ def tile_customconvmodule_s_kernel(tc, x, weight, bias, out):
         def regroup(v, b):
             h0 = v * CHUNK
             rows = rows_of(v)
-            copy = nc.scalar.copy if b == 1 and 0 < v < N_CHUNKS - 1 else nc.vector.tensor_copy
-            source = raw[v][:, b, :, 0 : rows * W].rearrange("p e (h w) -> p h w e", w=W)
-            copy(
-                out=grouped[:, h0 : h0 + rows, b, E : E + W * PACK].rearrange(
-                    "p h (w d e) -> p h w d e", d=KW, e=E
-                ),
-                in_=source.unsqueeze(3).to_broadcast([P, rows, W, KW, E]),
-            )
+            copy = nc.vector.tensor_copy
+            pixels = raw[v][:, b, :, 0 : rows * W].rearrange("p e (h w) -> p h w e", w=W)
+            target = grouped[:, h0 : h0 + rows, b]
+            for s in range(KW):
+                first = 1 - s
+                copy(
+                    out=target[:, :, s, first : first + HALF - 1],
+                    in_=pixels[:, :, first : first + W - 1].rearrange("p h (k j) e -> p h k e j", j=KW),
+                )
+            copy(out=target[:, :, 0, 0, :, 1], in_=pixels[:, :, 0])
+            copy(out=target[:, :, 1, HALF - 1, :, 0], in_=pixels[:, :, W - 1])
 
         def quantise(h0, rows):
             first = (h0 + 1) * ROW
             nc.vector.quantize_mx(
                 out=x_codes[:, first : first + rows * ROW].bitcast(FP8X4),
                 scales=x_scales[:, first : first + rows * ROW],
-                in_=grouped[:, h0 : h0 + rows].rearrange("p h b f -> p (h b f)"),
+                in_=grouped[:, h0 : h0 + rows].rearrange("p h b s k e j -> p (h b s k e j)"),
             )
 
         def multiply_and_store(h0, rows):
@@ -90,12 +93,13 @@ def tile_customconvmodule_s_kernel(tc, x, weight, bias, out):
                     stop=(i == KH - 1),
                 )
             result = results.tile([O, B, rows, WO], F32, name="result")
-            nc.scalar.activation(
-                out=result[:],
-                in_=acc[:].rearrange("o (y b z) -> o b y z", b=B, z=WO),
-                func=mybir.ActivationFunctionType.Identity,
-                bias=bias_col[:, 0:1],
-            )
+            for b in range(B):
+                nc.scalar.activation(
+                    out=result[:, b].rearrange("o y (k s) -> o y k s", s=KW),
+                    in_=acc[:].rearrange("o (y b s k) -> o b y k s", b=B, s=KW, k=HALF)[:, b],
+                    func=mybir.ActivationFunctionType.Identity,
+                    bias=bias_col[:, 0:1],
+                )
             nc.sync.dma_start(
                 out=out.rearrange("b o y z -> o b (y z)")[:, :, h0 * WO : (h0 + rows) * WO],
                 in_=result[:].rearrange("o b y z -> o b (y z)"),
@@ -111,9 +115,9 @@ def tile_customconvmodule_s_kernel(tc, x, weight, bias, out):
         nc.scalar.activation(out=warm[:], in_=warm[:], func=mybir.ActivationFunctionType.Identity)
         make_identity(nc, ident[:])
         nc.gpsimd.tensor_copy(out=bias_rows[0:1, :], in_=bias_row[:])
-        nc.vector.memset(grouped[:, :, :, 0:EDGE], 0.0)
-        nc.vector.memset(grouped[:, :, :, WO * PACK - EDGE : WO * PACK], 0.0)
-        nc.vector.memset(grouped[:, H, :, :], 0.0)
+        nc.vector.memset(grouped[:, :, :, 0, 0], 0.0)
+        nc.vector.memset(grouped[:, :, :, 1, HALF - 1], 0.0)
+        nc.vector.memset(grouped[:, H], 0.0)
         nc.vector.memset(x_codes[:, 0:ROW].bitcast(I32), 0)
         nc.vector.memset(x_scales[:, 0:ROW].bitcast(I32), 0)
 
@@ -127,14 +131,14 @@ def tile_customconvmodule_s_kernel(tc, x, weight, bias, out):
 
         def copy_weight_out():
             for i in range(KH):
-                nc.scalar.copy(out=w_grouped[:, i], in_=w_turned[i][:].bitcast(BF16).rearrange("p e (o j) -> p o j e", j=KW))
+                nc.scalar.copy(out=w_grouped[:, i].rearrange("p o e j -> p o (e j)").bitcast(F32), in_=w_turned[i][:].rearrange("p e o -> p o e"))
             nc.scalar.copy(out=bias_col[:], in_=bias_turned[:, 0:1])
 
         def quantise_weight():
             nc.vector.quantize_mx(
                 out=w_codes[:].bitcast(FP8X4),
                 scales=w_scales[:],
-                in_=w_grouped[:].rearrange("p i o j e -> p (i o j e)"),
+                in_=w_grouped[:].rearrange("p i o e j -> p (i o e j)"),
             )
 
         for v in range(N_CHUNKS + 1):

@@ -14,11 +14,13 @@ O, KH, KW = 128, 2, 2
 HO, WO = 32, 32
 E = C // P
 PACK = KW * E
-ROW = B * WO
-CHUNK = 8
-N_CHUNKS = HO // CHUNK
-N_TILE = CHUNK * ROW
 HALF = WO // 2
+ROW = B * WO
+CHUNK = 16
+N_CHUNKS = HO // CHUNK
+PAIRS = W // 2
+ON_VECTOR = (2, 4)
+EDGE_STEP = (WO - 1) * PACK - 1
 
 FLOPS = 2 * B * HO * WO * C * KH * KW * O
 STEPS = [(0, 8), (8, 8), (16, 8), (24, 4), (28, 4)]
@@ -26,61 +28,89 @@ STEPS = [(0, 8), (8, 8), (16, 8), (24, 4), (28, 4)]
 
 def tile_customconvmodule_s_kernel(tc, x, weight, bias, out):
     nc = tc.nc
-    with tc.tile_pool(name="keep", bufs=1) as keep, tc.tile_pool(
-        name="results", bufs=len(STEPS)
-    ) as results, tc.psum_pool(name="turned", bufs=1) as turned, tc.psum_pool(
-        name="sums", bufs=4
+    with tc.tile_pool(name="keep", bufs=1) as keep, tc.psum_pool(name="turned", bufs=1) as turned, tc.psum_pool(
+        name="sums", bufs=1
     ) as sums, tc.manual_schedule():
-        raw = [keep.tile([P, B, E, CHUNK * W], BF16, name="raw%d" % v) for v in range(N_CHUNKS)]
+        raw = [
+            [keep.tile([P, E, CHUNK * W], BF16, name="raw%d_%d" % (v, b)) for b in range(B)] for v in range(N_CHUNKS)
+        ]
         w_rows = keep.tile([O, C * KH * KW], BF16)
         bias_row = keep.tile([1, O], BF16)
         bias_rows = keep.tile([P, P], F32)
         ident = keep.tile([P, P], F32)
         warm = keep.tile([P, 1], F32)
+        zeros = keep.tile([P, P], F32)
         grouped = keep.tile([P, HO, B, KW, HALF, E, KW], BF16, align_bytes=64)
+        grouped_flat = grouped[:].rearrange("p h b s k e j -> p (h b s k e j)")
         x_codes = keep.tile([P, (HO + 1) * ROW], U32, align_bytes=64)
         x_scales = keep.tile([P, (HO + 1) * ROW], U8, align_bytes=64)
         w_grouped = keep.tile([P, KH, O, E, KW], BF16, align_bytes=64)
         w_codes = keep.tile([P, KH * O], U32, align_bytes=64)
         w_scales = keep.tile([P, KH * O], U8, align_bytes=64)
         bias_col = keep.tile([P, 1], F32)
+        results = [keep.tile([O, B, rows, HALF, KW], F32, name="result%d" % h0) for h0, rows in STEPS]
 
         def rows_of(v):
             return min(CHUNK, H - v * CHUNK)
 
-        def load(v):
+        def load(v, b):
             first = v * CHUNK * W
-            for b in range(B):
-                nc.sync.dma_start(
-                    out=raw[v][:, b, :, 0 : rows_of(v) * W],
-                    in_=x[b].rearrange("(e p) h w -> p e (h w)", e=E)[:, :, first : first + rows_of(v) * W],
-                )
+            nc.sync.dma_start(
+                out=raw[v][b][:, :, 0 : rows_of(v) * W],
+                in_=x[b].rearrange("(e p) h w -> p e (h w)", e=E)[:, :, first : first + rows_of(v) * W],
+            )
 
-        def regroup(v, b):
+        def load_weight():
+            nc.sync.dma_start(out=w_rows[:], in_=weight.rearrange("o c i j -> o (c i j)"))
+
+        def target_of(v, b, q):
             h0 = v * CHUNK
-            rows = rows_of(v)
-            copy = nc.vector.tensor_copy
-            pixels = raw[v][:, b, :, 0 : rows * W].rearrange("p e (h w) -> p h w e", w=W)
-            target = grouped[:, h0 : h0 + rows, b]
-            for s in range(KW):
-                first = 1 - s
-                copy(
-                    out=target[:, :, s, first : first + HALF - 1],
-                    in_=pixels[:, :, first : first + W - 1].rearrange("p h (k j) e -> p h k e j", j=KW),
-                )
-            copy(out=target[:, :, 0, 0, :, 1], in_=pixels[:, :, 0])
-            copy(out=target[:, :, 1, HALF - 1, :, 0], in_=pixels[:, :, W - 1])
+            return grouped[:, h0 + q : h0 + rows_of(v) : 2, b]
 
-        def quantise(h0, rows):
-            first = (h0 + 1) * ROW
+        def regroup_words(v, b):
+            words = raw[v][b][:].bitcast(F32).rearrange("p e (r c) -> p r c e", c=W)
+            for q in range(2):
+                rows = (rows_of(v) + 1 - q) // 2
+                first = q * (PAIRS + 1)
+                nc.scalar.copy(
+                    out=target_of(v, b, q)[:, :, 1 - q, q : q + PAIRS]
+                    .rearrange("p r k e j -> p r k (e j)")
+                    .bitcast(F32),
+                    in_=words[:, 0:rows, first : first + PAIRS],
+                )
+
+        def regroup_pairs(v, b):
+            pixels = raw[v][b][:].rearrange("p e (h w) -> p h w e", w=W)
+            for q in range(2):
+                first = 1 - q
+                nc.vector.tensor_copy(
+                    out=target_of(v, b, q)[:, :, q, first : first + PAIRS],
+                    in_=pixels[:, q : rows_of(v) : 2, first : first + 2 * PAIRS].rearrange(
+                        "p r (k j) e -> p r k e j", j=KW
+                    ),
+                )
+
+        def regroup_edges(v, b, copy):
+            start = (v * CHUNK * B + b) * WO * PACK + 1
+            rows = rows_of(v)
+            edges = grouped_flat[:, start : start + rows * ROW * PACK].rearrange("p (h f) -> p h f", h=rows)
+            copy(
+                out=edges[:, :, 0 : 2 * EDGE_STEP].rearrange("p h (g r) -> p h g r", g=2)[:, :, :, 0 : KW * E : KW],
+                in_=raw[v][b][:, :, 0 : rows * W].rearrange("p e (h w) -> p h w e", w=W)[:, :, 0 : W : W - 1],
+            )
+
+        def quantise(n):
+            h0, rows = STEPS[n]
+            columns = slice((h0 + 1) * ROW, (h0 + 1 + rows) * ROW)
             nc.vector.quantize_mx(
-                out=x_codes[:, first : first + rows * ROW].bitcast(FP8X4),
-                scales=x_scales[:, first : first + rows * ROW],
+                out=x_codes[:, columns].bitcast(FP8X4),
+                scales=x_scales[:, columns],
                 in_=grouped[:, h0 : h0 + rows].rearrange("p h b s k e j -> p (h b s k e j)"),
             )
 
-        def multiply_and_store(h0, rows):
-            acc = sums.tile([O, rows * ROW], F32, name="acc")
+        def multiply(n):
+            h0, rows = STEPS[n]
+            acc = sums.tile([O, rows * ROW], F32, name="acc%d" % n)
             for i in range(KH):
                 window = slice((h0 + i) * ROW, (h0 + i + rows) * ROW)
                 nc.tensor.matmul_mx(
@@ -92,28 +122,46 @@ def tile_customconvmodule_s_kernel(tc, x, weight, bias, out):
                     start=(i == 0),
                     stop=(i == KH - 1),
                 )
-            result = results.tile([O, B, rows, WO], F32, name="result")
+            return acc[:].rearrange("o (y b s k) -> o b y k s", b=B, s=KW, k=HALF)
+
+        def empty_on_scalar(n, acc):
             for b in range(B):
                 nc.scalar.activation(
-                    out=result[:, b].rearrange("o y (k s) -> o y k s", s=KW),
-                    in_=acc[:].rearrange("o (y b s k) -> o b y k s", b=B, s=KW, k=HALF)[:, b],
+                    out=results[n][:, b],
+                    in_=acc[:, b],
                     func=mybir.ActivationFunctionType.Identity,
                     bias=bias_col[:, 0:1],
                 )
+
+        def empty_on_vector(n, acc):
+            for b in range(B):
+                nc.vector.tensor_scalar(
+                    out=results[n][:, b],
+                    in0=acc[:, b],
+                    scalar1=bias_col[:, 0:1],
+                    scalar2=None,
+                    op0=mybir.AluOpType.add,
+                )
+
+        def store(n):
+            h0, rows = STEPS[n]
             nc.sync.dma_start(
                 out=out.rearrange("b o y z -> o b (y z)")[:, :, h0 * WO : (h0 + rows) * WO],
-                in_=result[:].rearrange("o b y z -> o b (y z)"),
+                in_=results[n][:].rearrange("o b y k s -> o b (y k s)"),
             )
 
-        nc.sync.dma_start(out=w_rows[:], in_=weight.rearrange("o c i j -> o (c i j)"))
-        for v in range(N_CHUNKS):
-            load(v)
-        nc.vector.memset(bias_rows[:], 0.0)
+        load(0, 0)
+        load(0, 1)
+        load_weight()
+        load(1, 0)
+        load(1, 1)
         nc.scalar.dma_start(out=bias_row[:], in_=bias.rearrange("(u o) -> u o", u=1))
 
         nc.vector.memset(warm[:], 0.0)
+        nc.vector.memset(zeros[:], 0.0)
         nc.scalar.activation(out=warm[:], in_=warm[:], func=mybir.ActivationFunctionType.Identity)
         make_identity(nc, ident[:])
+        nc.vector.memset(bias_rows[:], 0.0)
         nc.gpsimd.tensor_copy(out=bias_rows[0:1, :], in_=bias_row[:])
         nc.vector.memset(grouped[:, :, :, 0, 0], 0.0)
         nc.vector.memset(grouped[:, :, :, 1, HALF - 1], 0.0)
@@ -121,18 +169,24 @@ def tile_customconvmodule_s_kernel(tc, x, weight, bias, out):
         nc.vector.memset(x_codes[:, 0:ROW].bitcast(I32), 0)
         nc.vector.memset(x_scales[:, 0:ROW].bitcast(I32), 0)
 
+        idle = turned.tile([P, P], F32)
+        for n in range(5):
+            nc.tensor.matmul(idle[:], lhsT=zeros[:], rhs=zeros[:], start=True, stop=True)
+
         w_pairs = w_rows[:].bitcast(F32).rearrange("o (e p i) -> o e i p", e=E, i=KH)
         w_turned = [turned.tile([P, E, O], F32, name="w_turned%d" % i) for i in range(KH)]
         for i in range(KH):
             for e in range(E):
                 nc.tensor.transpose(w_turned[i][:, e, :], w_pairs[:, e, i, :], ident[:])
-        bias_turned = turned.tile([P, P], F32)
-        nc.tensor.transpose(bias_turned[:], bias_rows[:], ident[:])
+        nc.tensor.transpose(idle[:], bias_rows[:], ident[:])
 
         def copy_weight_out():
             for i in range(KH):
-                nc.scalar.copy(out=w_grouped[:, i].rearrange("p o e j -> p o (e j)").bitcast(F32), in_=w_turned[i][:].rearrange("p e o -> p o e"))
-            nc.scalar.copy(out=bias_col[:], in_=bias_turned[:, 0:1])
+                nc.scalar.copy(
+                    out=w_grouped[:, i].rearrange("p o e j -> p o (e j)").bitcast(F32),
+                    in_=w_turned[i][:].rearrange("p e o -> p o e"),
+                )
+            nc.scalar.copy(out=bias_col[:], in_=idle[:, 0:1])
 
         def quantise_weight():
             nc.vector.quantize_mx(
@@ -141,17 +195,27 @@ def tile_customconvmodule_s_kernel(tc, x, weight, bias, out):
                 in_=w_grouped[:].rearrange("p i o e j -> p (i o e j)"),
             )
 
-        for v in range(N_CHUNKS + 1):
-            if v < N_CHUNKS:
-                regroup(v, 0)
-            for h0, rows in STEPS:
-                if h0 // CHUNK == v - 1:
-                    quantise(h0, rows)
-            if v == 0:
-                copy_weight_out()
-            if v == 1:
-                quantise_weight()
-            if v < N_CHUNKS:
-                regroup(v, 1)
-        for h0, rows in STEPS:
-            multiply_and_store(h0, rows)
+        regroup_words(0, 0)
+        regroup_words(0, 1)
+        copy_weight_out()
+        regroup_words(1, 0)
+        regroup_words(1, 1)
+        for b in range(B):
+            regroup_pairs(0, b)
+            regroup_edges(0, b, nc.vector.tensor_copy)
+        quantise(0)
+        quantise(1)
+        regroup_pairs(1, 0)
+        regroup_edges(1, 0, nc.vector.tensor_copy)
+        quantise_weight()
+        regroup_pairs(1, 1)
+        regroup_edges(1, 1, nc.vector.tensor_copy)
+        for n in range(2, len(STEPS)):
+            quantise(n)
+        for n in range(len(STEPS)):
+            acc = multiply(n)
+            if n in ON_VECTOR:
+                empty_on_vector(n, acc)
+            else:
+                empty_on_scalar(n, acc)
+            store(n)

@@ -18,19 +18,18 @@ HALF = WO // 2
 ROW = B * WO
 CHUNK = 16
 N_CHUNKS = HO // CHUNK
+BANKS = 8
 PAIRS = W // 2
-ON_VECTOR = (2, 4)
+ON_VECTOR = (3, 5)
 EDGE_STEP = (WO - 1) * PACK - 1
 
 FLOPS = 2 * B * HO * WO * C * KH * KW * O
-STEPS = [(0, 8), (8, 8), (16, 8), (24, 4), (28, 4)]
+STEPS = [(0, 8), (8, 8), (16, 4), (20, 4), (24, 4), (28, 4)]
 
 
 def tile_customconvmodule_s_kernel(tc, x, weight, bias, out):
     nc = tc.nc
-    with tc.tile_pool(name="keep", bufs=1) as keep, tc.psum_pool(name="turned", bufs=1) as turned, tc.psum_pool(
-        name="sums", bufs=1
-    ) as sums, tc.manual_schedule():
+    with tc.tile_pool(name="keep", bufs=1) as keep, tc.psum_pool(name="psum", bufs=1) as psum, tc.manual_schedule():
         raw = [
             [keep.tile([P, E, CHUNK * W], BF16, name="raw%d_%d" % (v, b)) for b in range(B)] for v in range(N_CHUNKS)
         ]
@@ -90,6 +89,18 @@ def tile_customconvmodule_s_kernel(tc, x, weight, bias, out):
                     ),
                 )
 
+        def regroup_all_pairs(v, b):
+            h0 = v * CHUNK
+            pixels = raw[v][b][:].rearrange("p e (h w) -> p h w e", w=W)
+            for s in range(KW):
+                first = 1 - s
+                nc.vector.tensor_copy(
+                    out=grouped[:, h0 : h0 + rows_of(v), b, s, first : first + PAIRS],
+                    in_=pixels[:, 0 : rows_of(v), first : first + 2 * PAIRS].rearrange(
+                        "p h (k j) e -> p h k e j", j=KW
+                    ),
+                )
+
         def regroup_edges(v, b, copy):
             start = (v * CHUNK * B + b) * WO * PACK + 1
             rows = rows_of(v)
@@ -110,7 +121,7 @@ def tile_customconvmodule_s_kernel(tc, x, weight, bias, out):
 
         def multiply(n):
             h0, rows = STEPS[n]
-            acc = sums.tile([O, rows * ROW], F32, name="acc%d" % n)
+            acc = psum.tile([O, rows * ROW], F32, name="acc%d" % n, tag="bank%d" % ((n + 3) % BANKS))
             for i in range(KH):
                 window = slice((h0 + i) * ROW, (h0 + i + rows) * ROW)
                 nc.tensor.matmul_mx(
@@ -151,8 +162,8 @@ def tile_customconvmodule_s_kernel(tc, x, weight, bias, out):
             )
 
         load(0, 0)
-        load(0, 1)
         load_weight()
+        load(0, 1)
         load(1, 0)
         load(1, 1)
         nc.scalar.dma_start(out=bias_row[:], in_=bias.rearrange("(u o) -> u o", u=1))
@@ -169,16 +180,22 @@ def tile_customconvmodule_s_kernel(tc, x, weight, bias, out):
         nc.vector.memset(x_codes[:, 0:ROW].bitcast(I32), 0)
         nc.vector.memset(x_scales[:, 0:ROW].bitcast(I32), 0)
 
-        idle = turned.tile([P, P], F32)
-        for n in range(5):
-            nc.tensor.matmul(idle[:], lhsT=zeros[:], rhs=zeros[:], start=True, stop=True)
+        idle = psum.tile([P, P], F32, name="idle", tag="bank2")
+
+        def keep_warm(times):
+            for n in range(times):
+                nc.tensor.matmul(idle[:], lhsT=zeros[:], rhs=zeros[:], start=True, stop=True)
+
+        keep_warm(5)
 
         w_pairs = w_rows[:].bitcast(F32).rearrange("o (e p i) -> o e i p", e=E, i=KH)
-        w_turned = [turned.tile([P, E, O], F32, name="w_turned%d" % i) for i in range(KH)]
+        w_turned = [psum.tile([P, E, O], F32, name="w_turned%d" % i, tag="bank%d" % i) for i in range(KH)]
         for i in range(KH):
             for e in range(E):
                 nc.tensor.transpose(w_turned[i][:, e, :], w_pairs[:, e, i, :], ident[:])
-        nc.tensor.transpose(idle[:], bias_rows[:], ident[:])
+        bias_turned = psum.tile([P, P], F32, name="bias_turned", tag="bank%d" % (BANKS - 1))
+        nc.tensor.transpose(bias_turned[:], bias_rows[:], ident[:])
+        keep_warm(2)
 
         def copy_weight_out():
             for i in range(KH):
@@ -186,7 +203,7 @@ def tile_customconvmodule_s_kernel(tc, x, weight, bias, out):
                     out=w_grouped[:, i].rearrange("p o e j -> p o (e j)").bitcast(F32),
                     in_=w_turned[i][:].rearrange("p e o -> p o e"),
                 )
-            nc.scalar.copy(out=bias_col[:], in_=idle[:, 0:1])
+            nc.scalar.copy(out=bias_col[:], in_=bias_turned[:, 0:1])
 
         def quantise_weight():
             nc.vector.quantize_mx(
@@ -195,21 +212,19 @@ def tile_customconvmodule_s_kernel(tc, x, weight, bias, out):
                 in_=w_grouped[:].rearrange("p i o e j -> p (i o e j)"),
             )
 
-        regroup_words(0, 0)
-        regroup_words(0, 1)
-        copy_weight_out()
-        regroup_words(1, 0)
-        regroup_words(1, 1)
         for b in range(B):
-            regroup_pairs(0, b)
-            regroup_edges(0, b, nc.vector.tensor_copy)
+            regroup_edges(0, b, nc.scalar.copy)
+        copy_weight_out()
+        for b in range(B):
+            regroup_words(1, b)
+            regroup_edges(1, b, nc.scalar.copy)
+        for b in range(B):
+            regroup_all_pairs(0, b)
         quantise(0)
-        quantise(1)
-        regroup_pairs(1, 0)
-        regroup_edges(1, 0, nc.vector.tensor_copy)
         quantise_weight()
-        regroup_pairs(1, 1)
-        regroup_edges(1, 1, nc.vector.tensor_copy)
+        quantise(1)
+        for b in range(B):
+            regroup_pairs(1, b)
         for n in range(2, len(STEPS)):
             quantise(n)
         for n in range(len(STEPS)):

@@ -34,8 +34,8 @@ def tile_customconvmodule_s_kernel(tc, x, weight, bias, out):
             [keep.tile([P, E, CHUNK * W], BF16, name="raw%d_%d" % (v, b)) for b in range(B)] for v in range(N_CHUNKS)
         ]
         w_rows = keep.tile([O, C * KH * KW], BF16)
-        bias_row = keep.tile([1, O], BF16)
-        bias_rows = keep.tile([P, P], F32)
+        bias_rows = keep.tile([P, O], BF16)
+        ones = keep.tile([P, KW], BF16)
         ident = keep.tile([P, P], F32)
         warm = keep.tile([P, 1], F32)
         zeros = keep.tile([P, P], F32)
@@ -166,14 +166,14 @@ def tile_customconvmodule_s_kernel(tc, x, weight, bias, out):
         load(0, 1)
         load(1, 0)
         load(1, 1)
-        nc.scalar.dma_start(out=bias_row[:], in_=bias.rearrange("(u o) -> u o", u=1))
 
-        nc.vector.memset(warm[:], 0.0)
+        nc.vector.memset(bias_rows[:], 0.0)
+        nc.scalar.dma_start(out=bias_rows[0:1, :], in_=bias.rearrange("(u o) -> u o", u=1))
         nc.vector.memset(zeros[:], 0.0)
+        nc.vector.memset(warm[:], 0.0)
         nc.scalar.activation(out=warm[:], in_=warm[:], func=mybir.ActivationFunctionType.Identity)
         make_identity(nc, ident[:])
-        nc.vector.memset(bias_rows[:], 0.0)
-        nc.gpsimd.tensor_copy(out=bias_rows[0:1, :], in_=bias_row[:])
+        nc.vector.memset(ones[:], 1.0)
         nc.vector.memset(grouped[:, :, :, 0, 0], 0.0)
         nc.vector.memset(grouped[:, :, :, 1, HALF - 1], 0.0)
         nc.vector.memset(grouped[:, H], 0.0)
@@ -193,8 +193,8 @@ def tile_customconvmodule_s_kernel(tc, x, weight, bias, out):
         for i in range(KH):
             for e in range(E):
                 nc.tensor.transpose(w_turned[i][:, e, :], w_pairs[:, e, i, :], ident[:])
-        bias_turned = psum.tile([P, P], F32, name="bias_turned", tag="bank%d" % (BANKS - 1))
-        nc.tensor.transpose(bias_turned[:], bias_rows[:], ident[:])
+        bias_turned = psum.tile([O, KW], F32, name="bias_turned", tag="bank%d" % (BANKS - 1))
+        nc.tensor.matmul(bias_turned[:], lhsT=bias_rows[:], rhs=ones[:], start=True, stop=True)
         keep_warm(2)
 
         def copy_weight_out():

@@ -195,7 +195,7 @@ def tile_customconvmodule_s_kernel(tc, x, weight, bias, out):
                 nc.tensor.transpose(w_turned[i][:, e, :], w_pairs[:, e, i, :], ident[:])
         bias_turned = psum.tile([O, KW], F32, name="bias_turned", tag="bank%d" % (BANKS - 1))
         nc.tensor.matmul(bias_turned[:], lhsT=bias_rows[:], rhs=ones[:], start=True, stop=True)
-        keep_warm(2)
+        keep_warm(4)
 
         def copy_weight_out():
             for i in range(KH):

@@ -18,6 +18,7 @@ HALF = WO // 2
 ROW = B * WO
 CHUNK = 16
 N_CHUNKS = HO // CHUNK
+PIECE = 512
 BANKS = 8
 PAIRS = W // 2
 ON_VECTOR = (3, 5)
@@ -31,8 +32,9 @@ def tile_customconvmodule_s_kernel(tc, x, weight, bias, out):
     nc = tc.nc
     with tc.tile_pool(name="keep", bufs=1) as keep, tc.psum_pool(name="psum", bufs=1) as psum, tc.manual_schedule():
         raw = [
-            [keep.tile([P, E, CHUNK * W], BF16, name="raw%d_%d" % (v, b)) for b in range(B)] for v in range(N_CHUNKS)
+            [keep.tile([P, E, PIECE], BF16, name="raw%d_%d" % (v, b)) for b in range(B)] for v in range(N_CHUNKS)
         ]
+        first_pixel = [0, H * W - PIECE]
         w_rows = keep.tile([O, C * KH * KW], BF16)
         bias_rows = keep.tile([P, O], BF16)
         ones = keep.tile([P, KW], BF16)
@@ -53,52 +55,53 @@ def tile_customconvmodule_s_kernel(tc, x, weight, bias, out):
             return min(CHUNK, H - v * CHUNK)
 
         def load(v, b):
-            first = v * CHUNK * W
             nc.sync.dma_start(
-                out=raw[v][b][:, :, 0 : rows_of(v) * W],
-                in_=x[b].rearrange("(e p) h w -> p e (h w)", e=E)[:, :, first : first + rows_of(v) * W],
+                out=raw[v][b][:],
+                in_=x[b].rearrange("(e p) h w -> p e (h w)", e=E)[:, :, first_pixel[v] : first_pixel[v] + PIECE],
             )
+
+        def pixels_of(v, b):
+            start = v * CHUNK * W - first_pixel[v]
+            return raw[v][b][:, :, start : start + rows_of(v) * W].rearrange("p e (h w) -> p h w e", w=W)
 
         def load_weight():
             nc.sync.dma_start(out=w_rows[:], in_=weight.rearrange("o c i j -> o (c i j)"))
 
-        def target_of(v, b, q):
-            h0 = v * CHUNK
-            return grouped[:, h0 + q : h0 + rows_of(v) : 2, b]
-
         def regroup_words(v, b):
-            words = raw[v][b][:].bitcast(F32).rearrange("p e (r c) -> p r c e", c=W)
+            start = v * CHUNK * W - first_pixel[v]
             for q in range(2):
+                s = (start + q + 1) % 2
+                first = 1 - s
                 rows = (rows_of(v) + 1 - q) // 2
-                first = q * (PAIRS + 1)
+                word = (start + q * W + first) // 2
+                skip = max(0, word + rows * W - PIECE // 2)
+                runs = raw[v][b][:].bitcast(F32)[:, :, word - skip : word - skip + rows * W]
                 nc.scalar.copy(
-                    out=target_of(v, b, q)[:, :, 1 - q, q : q + PAIRS]
+                    out=grouped[:, v * CHUNK + q : v * CHUNK + rows_of(v) : 2, b, s, first : first + PAIRS]
                     .rearrange("p r k e j -> p r k (e j)")
                     .bitcast(F32),
-                    in_=words[:, 0:rows, first : first + PAIRS],
+                    in_=runs.rearrange("p e (r c) -> p r c e", c=W)[:, :, skip : skip + PAIRS],
                 )
 
         def regroup_pairs(v, b):
-            pixels = raw[v][b][:].rearrange("p e (h w) -> p h w e", w=W)
+            start = v * CHUNK * W - first_pixel[v]
             for q in range(2):
-                first = 1 - q
+                s = (start + q) % 2
+                first = 1 - s
                 nc.vector.tensor_copy(
-                    out=target_of(v, b, q)[:, :, q, first : first + PAIRS],
-                    in_=pixels[:, q : rows_of(v) : 2, first : first + 2 * PAIRS].rearrange(
+                    out=grouped[:, v * CHUNK + q : v * CHUNK + rows_of(v) : 2, b, s, first : first + PAIRS],
+                    in_=pixels_of(v, b)[:, q : rows_of(v) : 2, first : first + 2 * PAIRS].rearrange(
                         "p r (k j) e -> p r k e j", j=KW
                     ),
                 )
 
         def regroup_all_pairs(v, b):
             h0 = v * CHUNK
-            pixels = raw[v][b][:].rearrange("p e (h w) -> p h w e", w=W)
             for s in range(KW):
                 first = 1 - s
                 nc.vector.tensor_copy(
                     out=grouped[:, h0 : h0 + rows_of(v), b, s, first : first + PAIRS],
-                    in_=pixels[:, 0 : rows_of(v), first : first + 2 * PAIRS].rearrange(
-                        "p h (k j) e -> p h k e j", j=KW
-                    ),
+                    in_=pixels_of(v, b)[:, :, first : first + 2 * PAIRS].rearrange("p h (k j) e -> p h k e j", j=KW),
                 )
 
         def regroup_edges(v, b, copy):
@@ -107,7 +110,7 @@ def tile_customconvmodule_s_kernel(tc, x, weight, bias, out):
             edges = grouped_flat[:, start : start + rows * ROW * PACK].rearrange("p (h f) -> p h f", h=rows)
             copy(
                 out=edges[:, :, 0 : 2 * EDGE_STEP].rearrange("p h (g r) -> p h g r", g=2)[:, :, :, 0 : KW * E : KW],
-                in_=raw[v][b][:, :, 0 : rows * W].rearrange("p e (h w) -> p h w e", w=W)[:, :, 0 : W : W - 1],
+                in_=pixels_of(v, b)[:, :, 0 : W : W - 1],
             )
 
         def quantise(n):

@@ -16,16 +16,17 @@ E = C // P
 PACK = KW * E
 HALF = WO // 2
 ROW = B * WO
-CHUNK = 16
+CHUNK = 8
 N_CHUNKS = HO // CHUNK
-PIECE = 512
+PIECE = 256
 BANKS = 8
 PAIRS = W // 2
-ON_VECTOR = (3, 5)
+SHARED = 2
+ON_VECTOR = 3
 EDGE_STEP = (WO - 1) * PACK - 1
 
 FLOPS = 2 * B * HO * WO * C * KH * KW * O
-STEPS = [(0, 8), (8, 8), (16, 4), (20, 4), (24, 4), (28, 4)]
+STEPS = [(0, 8), (8, 8), (16, 8), (24, 4), (28, 4)]
 
 
 def tile_customconvmodule_s_kernel(tc, x, weight, bias, out):
@@ -34,7 +35,7 @@ def tile_customconvmodule_s_kernel(tc, x, weight, bias, out):
         raw = [
             [keep.tile([P, E, PIECE], BF16, name="raw%d_%d" % (v, b)) for b in range(B)] for v in range(N_CHUNKS)
         ]
-        first_pixel = [0, H * W - PIECE]
+        first_pixel = [min(v * CHUNK * W, H * W - PIECE) for v in range(N_CHUNKS)]
         w_rows = keep.tile([O, C * KH * KW], BF16)
         bias_rows = keep.tile([P, O], BF16)
         ones = keep.tile([P, KW], BF16)
@@ -157,6 +158,14 @@ def tile_customconvmodule_s_kernel(tc, x, weight, bias, out):
                     op0=mybir.AluOpType.add,
                 )
 
+        def multiply_and_store(n):
+            acc = multiply(n)
+            if n == ON_VECTOR:
+                empty_on_vector(n, acc)
+            else:
+                empty_on_scalar(n, acc)
+            store(n)
+
         def store(n):
             h0, rows = STEPS[n]
             nc.sync.dma_start(
@@ -164,11 +173,12 @@ def tile_customconvmodule_s_kernel(tc, x, weight, bias, out):
                 in_=results[n][:].rearrange("o b y k s -> o b (y k s)"),
             )
 
-        load(0, 0)
+        for b in range(B):
+            load(0, b)
         load_weight()
-        load(0, 1)
-        load(1, 0)
-        load(1, 1)
+        for v in range(1, N_CHUNKS):
+            for b in range(B):
+                load(v, b)
 
         nc.vector.memset(bias_rows[:], 0.0)
         nc.scalar.dma_start(out=bias_rows[0:1, :], in_=bias.rearrange("(u o) -> u o", u=1))
@@ -215,25 +225,22 @@ def tile_customconvmodule_s_kernel(tc, x, weight, bias, out):
                 in_=w_grouped[:].rearrange("p i o e j -> p (i o e j)"),
             )
 
-        for b in range(B):
-            regroup_edges(0, b, nc.scalar.copy)
-        copy_weight_out()
-        for b in range(B):
-            regroup_words(1, b)
-            regroup_edges(1, b, nc.scalar.copy)
-        for b in range(B):
-            regroup_all_pairs(0, b)
-        quantise(0)
-        quantise_weight()
-        quantise(1)
-        for b in range(B):
-            regroup_pairs(1, b)
-        for n in range(2, len(STEPS)):
-            quantise(n)
-        for n in range(len(STEPS)):
-            acc = multiply(n)
-            if n in ON_VECTOR:
-                empty_on_vector(n, acc)
-            else:
-                empty_on_scalar(n, acc)
-            store(n)
+        for v in range(N_CHUNKS):
+            for b in range(B):
+                if v == SHARED:
+                    regroup_words(v, b)
+                    regroup_pairs(v, b)
+                else:
+                    regroup_all_pairs(v, b)
+                regroup_edges(v, b, nc.scalar.copy)
+            if v == 0:
+                copy_weight_out()
+            if v == 1:
+                quantise_weight()
+            if v == N_CHUNKS - 2:
+                multiply_and_store(0)
+            for n in range(len(STEPS)):
+                if STEPS[n][0] // CHUNK == v:
+                    quantise(n)
+        for n in range(1, len(STEPS)):
+            multiply_and_store(n)

import concourse.mybir as mybir
from concourse.masks import make_identity

BF16 = mybir.dt.bfloat16
F32 = mybir.dt.float32
I32 = mybir.dt.int32
U32 = mybir.dt.uint32
U8 = mybir.dt.uint8
FP8X4 = mybir.dt.float8_e4m3fn_x4

P = 128
B, C, H, W = 2, 256, 31, 31
O, KH, KW = 128, 2, 2
HO, WO = 32, 32
E = C // P
PACK = KW * E
HALF = WO // 2
ROW = B * WO
CHUNK = 8
N_CHUNKS = HO // CHUNK
PIECE = 256
BANKS = 8
PAIRS = W // 2
SHARED = 2
ON_VECTOR = 3
EDGE_STEP = (WO - 1) * PACK - 1

FLOPS = 2 * B * HO * WO * C * KH * KW * O
STEPS = [(0, 8), (8, 8), (16, 8), (24, 4), (28, 4)]


def tile_customconvmodule_s_kernel(tc, x, weight, bias, out):
    nc = tc.nc
    with tc.tile_pool(name="keep", bufs=1) as keep, tc.psum_pool(name="psum", bufs=1) as psum, tc.manual_schedule():
        raw = [
            [keep.tile([P, E, PIECE], BF16, name="raw%d_%d" % (v, b)) for b in range(B)] for v in range(N_CHUNKS)
        ]
        first_pixel = [min(v * CHUNK * W, H * W - PIECE) for v in range(N_CHUNKS)]
        w_rows = keep.tile([O, C * KH * KW], BF16)
        bias_rows = keep.tile([P, O], BF16)
        ones = keep.tile([P, KW], BF16)
        ident = keep.tile([P, P], F32)
        warm = keep.tile([P, 1], F32)
        zeros = keep.tile([P, P], F32)
        grouped = keep.tile([P, HO, B, KW, HALF, E, KW], BF16, align_bytes=64)
        grouped_flat = grouped[:].rearrange("p h b s k e j -> p (h b s k e j)")
        x_codes = keep.tile([P, (HO + 1) * ROW], U32, align_bytes=64)
        x_scales = keep.tile([P, (HO + 1) * ROW], U8, align_bytes=64)
        w_grouped = keep.tile([P, KH, O, E, KW], BF16, align_bytes=64)
        w_codes = keep.tile([P, KH * O], U32, align_bytes=64)
        w_scales = keep.tile([P, KH * O], U8, align_bytes=64)
        bias_col = keep.tile([P, 1], F32)
        results = [keep.tile([O, B, rows, HALF, KW], F32, name="result%d" % h0) for h0, rows in STEPS]

        def rows_of(v):
            return min(CHUNK, H - v * CHUNK)

        def load(v, b):
            nc.sync.dma_start(
                out=raw[v][b][:],
                in_=x[b].rearrange("(e p) h w -> p e (h w)", e=E)[:, :, first_pixel[v] : first_pixel[v] + PIECE],
            )

        def pixels_of(v, b):
            start = v * CHUNK * W - first_pixel[v]
            return raw[v][b][:, :, start : start + rows_of(v) * W].rearrange("p e (h w) -> p h w e", w=W)

        def load_weight():
            nc.sync.dma_start(out=w_rows[:], in_=weight.rearrange("o c i j -> o (c i j)"))

        def regroup_words(v, b):
            start = v * CHUNK * W - first_pixel[v]
            for q in range(2):
                s = (start + q + 1) % 2
                first = 1 - s
                rows = (rows_of(v) + 1 - q) // 2
                word = (start + q * W + first) // 2
                skip = max(0, word + rows * W - PIECE // 2)
                runs = raw[v][b][:].bitcast(F32)[:, :, word - skip : word - skip + rows * W]
                nc.scalar.copy(
                    out=grouped[:, v * CHUNK + q : v * CHUNK + rows_of(v) : 2, b, s, first : first + PAIRS]
                    .rearrange("p r k e j -> p r k (e j)")
                    .bitcast(F32),
                    in_=runs.rearrange("p e (r c) -> p r c e", c=W)[:, :, skip : skip + PAIRS],
                )

        def regroup_pairs(v, b):
            start = v * CHUNK * W - first_pixel[v]
            for q in range(2):
                s = (start + q) % 2
                first = 1 - s
                nc.vector.tensor_copy(
                    out=grouped[:, v * CHUNK + q : v * CHUNK + rows_of(v) : 2, b, s, first : first + PAIRS],
                    in_=pixels_of(v, b)[:, q : rows_of(v) : 2, first : first + 2 * PAIRS].rearrange(
                        "p r (k j) e -> p r k e j", j=KW
                    ),
                )

        def regroup_all_pairs(v, b):
            h0 = v * CHUNK
            for s in range(KW):
                first = 1 - s
                nc.vector.tensor_copy(
                    out=grouped[:, h0 : h0 + rows_of(v), b, s, first : first + PAIRS],
                    in_=pixels_of(v, b)[:, :, first : first + 2 * PAIRS].rearrange("p h (k j) e -> p h k e j", j=KW),
                )

        def regroup_edges(v, b, copy):
            start = (v * CHUNK * B + b) * WO * PACK + 1
            rows = rows_of(v)
            edges = grouped_flat[:, start : start + rows * ROW * PACK].rearrange("p (h f) -> p h f", h=rows)
            copy(
                out=edges[:, :, 0 : 2 * EDGE_STEP].rearrange("p h (g r) -> p h g r", g=2)[:, :, :, 0 : KW * E : KW],
                in_=pixels_of(v, b)[:, :, 0 : W : W - 1],
            )

        def quantise(n):
            h0, rows = STEPS[n]
            columns = slice((h0 + 1) * ROW, (h0 + 1 + rows) * ROW)
            nc.vector.quantize_mx(
                out=x_codes[:, columns].bitcast(FP8X4),
                scales=x_scales[:, columns],
                in_=grouped[:, h0 : h0 + rows].rearrange("p h b s k e j -> p (h b s k e j)"),
            )

        def multiply(n):
            h0, rows = STEPS[n]
            acc = psum.tile([O, rows * ROW], F32, name="acc%d" % n, tag="bank%d" % ((n + 3) % BANKS))
            for i in range(KH):
                window = slice((h0 + i) * ROW, (h0 + i + rows) * ROW)
                nc.tensor.matmul_mx(
                    out=acc[:],
                    lhsT=w_codes[:, i * O : (i + 1) * O].bitcast(FP8X4),
                    lhsT_scale=w_scales[:, i * O : (i + 1) * O],
                    rhs=x_codes[:, window].bitcast(FP8X4),
                    rhs_scale=x_scales[:, window],
                    start=(i == 0),
                    stop=(i == KH - 1),
                )
            return acc[:].rearrange("o (y b s k) -> o b y k s", b=B, s=KW, k=HALF)

        def empty_on_scalar(n, acc):
            for b in range(B):
                nc.scalar.activation(
                    out=results[n][:, b],
                    in_=acc[:, b],
                    func=mybir.ActivationFunctionType.Identity,
                    bias=bias_col[:, 0:1],
                )

        def empty_on_vector(n, acc):
            for b in range(B):
                nc.vector.tensor_scalar(
                    out=results[n][:, b],
                    in0=acc[:, b],
                    scalar1=bias_col[:, 0:1],
                    scalar2=None,
                    op0=mybir.AluOpType.add,
                )

        def multiply_and_store(n):
            acc = multiply(n)
            if n == ON_VECTOR:
                empty_on_vector(n, acc)
            else:
                empty_on_scalar(n, acc)
            store(n)

        def store(n):
            h0, rows = STEPS[n]
            nc.sync.dma_start(
                out=out.rearrange("b o y z -> o b (y z)")[:, :, h0 * WO : (h0 + rows) * WO],
                in_=results[n][:].rearrange("o b y k s -> o b (y k s)"),
            )

        for b in range(B):
            load(0, b)
        load_weight()
        for v in range(1, N_CHUNKS):
            for b in range(B):
                load(v, b)

        nc.vector.memset(bias_rows[:], 0.0)
        nc.scalar.dma_start(out=bias_rows[0:1, :], in_=bias.rearrange("(u o) -> u o", u=1))
        nc.vector.memset(zeros[:], 0.0)
        nc.vector.memset(warm[:], 0.0)
        nc.scalar.activation(out=warm[:], in_=warm[:], func=mybir.ActivationFunctionType.Identity)
        make_identity(nc, ident[:])
        nc.vector.memset(ones[:], 1.0)
        nc.vector.memset(grouped[:, :, :, 0, 0], 0.0)
        nc.vector.memset(grouped[:, :, :, 1, HALF - 1], 0.0)
        nc.vector.memset(grouped[:, H], 0.0)
        nc.vector.memset(x_codes[:, 0:ROW].bitcast(I32), 0)
        nc.vector.memset(x_scales[:, 0:ROW].bitcast(I32), 0)

        idle = psum.tile([P, P], F32, name="idle", tag="bank2")

        def keep_warm(times):
            for n in range(times):
                nc.tensor.matmul(idle[:], lhsT=zeros[:], rhs=zeros[:], start=True, stop=True)

        keep_warm(5)

        w_pairs = w_rows[:].bitcast(F32).rearrange("o (e p i) -> o e i p", e=E, i=KH)
        w_turned = [psum.tile([P, E, O], F32, name="w_turned%d" % i, tag="bank%d" % i) for i in range(KH)]
        for i in range(KH):
            for e in range(E):
                nc.tensor.transpose(w_turned[i][:, e, :], w_pairs[:, e, i, :], ident[:])
        bias_turned = psum.tile([O, KW], F32, name="bias_turned", tag="bank%d" % (BANKS - 1))
        nc.tensor.matmul(bias_turned[:], lhsT=bias_rows[:], rhs=ones[:], start=True, stop=True)
        keep_warm(4)

        def copy_weight_out():
            for i in range(KH):
                nc.scalar.copy(
                    out=w_grouped[:, i].rearrange("p o e j -> p o (e j)").bitcast(F32),
                    in_=w_turned[i][:].rearrange("p e o -> p o e"),
                )
            nc.scalar.copy(out=bias_col[:], in_=bias_turned[:, 0:1])

        def quantise_weight():
            nc.vector.quantize_mx(
                out=w_codes[:].bitcast(FP8X4),
                scales=w_scales[:],
                in_=w_grouped[:].rearrange("p i o e j -> p (i o e j)"),
            )

        for v in range(N_CHUNKS):
            for b in range(B):
                if v == SHARED:
                    regroup_words(v, b)
                    regroup_pairs(v, b)
                else:
                    regroup_all_pairs(v, b)
                regroup_edges(v, b, nc.scalar.copy)
            if v == 0:
                copy_weight_out()
            if v == 1:
                quantise_weight()
            if v == N_CHUNKS - 2:
                multiply_and_store(0)
            for n in range(len(STEPS)):
                if STEPS[n][0] // CHUNK == v:
                    quantise(n)
        for n in range(1, len(STEPS)):
            multiply_and_store(n)
